import numpy as np
import ml_dtypes


def mxq(x, axis, fmt="e4m3"):
    dtype, down = {"e4m3": (ml_dtypes.float8_e4m3fn, 7), "e5m2": (ml_dtypes.float8_e5m2, 14)}[fmt]
    v = np.moveaxis(np.asarray(x, np.float32).astype(ml_dtypes.bfloat16).astype(np.float64), axis, -1)
    blocks = v.reshape(v.shape[:-1] + (-1, 32))
    amax = np.abs(blocks).max(-1, keepdims=True)
    byte = np.maximum(np.where(amax > 0, np.frexp(amax)[1] - 1 + 127, 0) - down, 1)
    scale = np.exp2(byte - 127.0)
    codes = (blocks / scale).astype(np.float32).astype(dtype).astype(np.float64)
    return np.moveaxis((codes * scale).reshape(v.shape), -1, axis)


WIDE = False


def mx_kscale(k):
    if not WIDE:
        return np.ones(k)
    levels = np.array([18, -18])
    if k % 512:
        return np.exp2(np.random.permutation(np.resize(levels, k // 32))).repeat(32)
    a = np.empty((k // 512, 16))
    for p in range(k // 512):
        a[p, :8] = np.random.permutation(np.resize(levels, 8))
        for g in range(8):
            far = levels[np.abs(levels - a[p, g]) >= 10]
            a[p, g + 8] = far[np.random.randint(len(far))]
    return np.exp2(a.ravel()).repeat(32)


BF16 = ml_dtypes.bfloat16


def bf(x):
    return np.asarray(x, np.float32).astype(BF16)


def f64(x):
    return np.asarray(x).astype(np.float64)


B, S, H, E, D = 1, 1024, 1024, 1216, 128
J = 2 * E + D


def sigmoid(t):
    return 1.0 / (1.0 + np.exp(-t))


def rotary_back(g, sin, cos):
    g1, g2 = g[:, :D // 2], g[:, D // 2:]
    even = g1 * cos + g2 * sin
    odd = g2 * cos - g1 * sin
    return np.stack([even, odd], axis=-1).reshape(g.shape[0], D)


def setup_inputs():
    s = mx_kscale(S)[:, None]
    u = mx_kscale(J)
    ur = np.concatenate([u[2 * E::2], u[2 * E::2]])
    pos = np.arange(S)[:, None]
    inv = np.exp(-np.arange(0, D, 2) / D * np.log(10000.0))
    ang = pos * inv[None, :]
    x0 = bf(np.random.standard_normal((B, S, H)))
    w0 = bf(np.random.standard_normal((H, J)) / np.sqrt(H))
    q_scale = bf(1.0 + 0.1 * np.random.standard_normal(D))
    k_scale = bf(1.0 + 0.1 * np.random.standard_normal(D))
    g0 = bf(np.random.standard_normal((B, S, E)) * np.exp2(np.random.randint(-6, 1, (B, S, 1))) / s * u[:E])
    g1 = bf(np.random.standard_normal((B, S, E)) * np.exp2(np.random.randint(-6, 1, (B, S, 1))) / s * u[E:2 * E])
    g2 = bf(np.random.standard_normal((B, S, D)) * np.exp2(np.random.randint(-6, 1, (B, S, 1))) / s * ur)
    g3 = bf(np.random.standard_normal((B, S, D)) * np.exp2(np.random.randint(-6, 1, (B, S, 1))) / s * ur)
    z = f64(x0) @ f64(w0)
    return {"hidden_states": bf(f64(x0) * s),
            "sin": bf(np.sin(ang)[None]),
            "cos": bf(np.cos(ang)[None]),
            "W_i": bf(f64(w0) / u),
            "q_scale": q_scale,
            "k_scale": k_scale,
            "z": np.asarray(z, np.float32),
            "grad_0": g0,
            "grad_1": g1,
            "grad_2": g2,
            "grad_3": g3}


def reference(hidden_states, sin, cos, W_i, q_scale, k_scale, z, grad_0, grad_1, grad_2, grad_3):
    x = f64(hidden_states).reshape(S, H)
    sn, cs = f64(sin)[0], f64(cos)[0]
    gu, gv = f64(grad_0).reshape(S, E), f64(grad_1).reshape(S, E)
    gq, gk = f64(grad_2).reshape(S, D), f64(grad_3).reshape(S, D)
    gqk = rotary_back(gq, sn, cs) * f64(q_scale) + rotary_back(gk, sn, cs) * f64(k_scale)
    zf = f64(z).reshape(S, J)
    sg = sigmoid(zf)
    dz = np.concatenate([gu, gv, gqk], axis=1) * (sg * (1.0 + zf * (1.0 - sg)))
    dx = mxq(dz, 1, "e5m2") @ mxq(f64(W_i), 1, "e4m3").T
    dw = mxq(x, 0, "e4m3").T @ mxq(dz, 0, "e5m2")
    return dx.reshape(B, S, H), dw

@@ -1,0 +1,368 @@
+from contextlib import ExitStack
+
+import concourse.mybir as mybir
+from concourse.masks import make_identity
+
+S, H, E, D = 1024, 1024, 1216, 128
+J = 2 * E + D
+FLOPS = 2 * 2 * S * H * J
+
+F32 = mybir.dt.float32
+BF16 = mybir.dt.bfloat16
+U32 = mybir.dt.uint32
+U8 = mybir.dt.uint8
+E4M3 = mybir.dt.float8_e4m3fn_x4
+E5M2 = mybir.dt.float8_e5m2_x4
+ALU = mybir.AluOpType
+ACT = mybir.ActivationFunctionType
+
+P = 128
+PACK = 4
+KP = P * PACK
+NG = S // KP
+NF = J // KP
+NU = NG * NF
+
+
+def tile_gatedattentionunit_pa_v_kernel(
+    tc, hidden_states, sin, cos, W_i, q_scale, k_scale, z, grad_0, grad_1, grad_2, grad_3, out_0, out_1
+):
+    nc = tc.nc
+    z_v = z.rearrange("b (g p j) w -> (b g) p j w", p=P, j=PACK)
+    x_v = hidden_states.rearrange("b (g p j) w -> (b g) p j w", p=P, j=PACK)
+    sin_v = sin.rearrange("b (g p j) w -> (b g) p j w", p=P, j=PACK)
+    cos_v = cos.rearrange("b (g p j) w -> (b g) p j w", p=P, j=PACK)
+    g_v = [t.rearrange("b (g p j) w -> (b g) p j w", p=P, j=PACK) for t in (grad_0, grad_1)]
+    qk_v = [t.rearrange("b (g p j) w -> (b g) p j w", p=P, j=PACK) for t in (grad_2, grad_3)]
+    w_v = W_i.rearrange("(a t p) k -> a p t k", p=P, t=4)
+    o0_v = out_0.rearrange("b (t p) h -> (b t) p h", p=P)
+    o1_v = out_1.rearrange("(t p) k -> t p k", p=P)
+
+    with ExitStack() as ctx:
+        keep = ctx.enter_context(tc.tile_pool(name="keep", bufs=1))
+        pool = ctx.enter_context(tc.tile_pool(name="pool", bufs=2))
+        psum = ctx.enter_context(tc.psum_pool(name="psum", bufs=2))
+
+        ident = keep.tile([P, P], F32, name="ident")
+        warm = keep.tile([P, 1], F32, name="warm")
+        w_codes = keep.tile([P, NF, H], U32, name="w_codes", align_bytes=64)
+        w_scales = keep.tile([P, NF, H], U8, name="w_scales", align_bytes=64)
+        x_codes = keep.tile([P, NG, H], U32, name="x_codes", align_bytes=64)
+        x_scales = keep.tile([P, NG, H], U8, name="x_scales", align_bytes=64)
+        f_codes = keep.tile([P, NF, S], U32, name="f_codes", align_bytes=64)
+        f_scales = keep.tile([P, NF, S], U8, name="f_scales", align_bytes=64)
+        sc_raw = keep.tile([P, 2, D], BF16, name="sc_raw")
+        sc = keep.tile([P, 2 * D], F32, name="sc")
+
+        zt, st, gt, dt_, raw, xraw, tcod, tscl, feat, gqk, qkt = {}, {}, {}, {}, {}, {}, {}, {}, {}, {}, {}
+        wfeat, xfeat, acc0 = {}, {}, {}
+
+        def bank_of(n, shape):
+            bank = psum.tile(shape, F32, name="bank", tag="b%d" % n, bufs=1)
+            return bank
+
+        def unit(k):
+            return k // NF, k % NF
+
+        def load_z(k, parts=1):
+            G, g = unit(k)
+            t = pool.tile([P, PACK, KP], F32, name="zt", tag="z", bufs=3)
+            zt[k] = t
+            w = KP // parts
+            for i in range(parts):
+                nc.sync.dma_start(out=t[:, :, i * w : (i + 1) * w], in_=z_v[G, :, :, g * KP + i * w : g * KP + (i + 1) * w])
+
+        def load_g(which, G):
+            t = pool.tile([P, PACK, E], BF16, name="gt", tag="g", bufs=3)
+            gt[which, G] = t
+            nc.sync.dma_start(out=t[:], in_=g_v[which][G])
+
+        w_order = [(0, 0), (0, 1), (0, 2), (0, 3), (0, 4), (1, 0), (1, 1), (1, 2), (1, 3), (1, 4)]
+
+        def load_w(s):
+            t = pool.tile([P, 4, 2 * KP], BF16, name="raw", tag="raw", bufs=3)
+            (a0, g0), (a1, g1) = w_order[2 * s], w_order[2 * s + 1]
+            if a0 == a1:
+                nc.sync.dma_start(out=t[:], in_=w_v[a0, :, :, g0 * KP : (g0 + 2) * KP])
+            else:
+                nc.sync.dma_start(out=t[:, :, :KP], in_=w_v[a0, :, :, g0 * KP : (g0 + 1) * KP])
+                nc.sync.dma_start(out=t[:, :, KP:], in_=w_v[a1, :, :, g1 * KP : (g1 + 1) * KP])
+            raw[a0, g0] = (t, 0)
+            raw[a1, g1] = (t, 1)
+
+        def load_x(G):
+            t = pool.tile([P, PACK, H], BF16, name="raw", tag="raw", bufs=3)
+            xraw[G] = t
+            nc.sync.dma_start(out=t[:], in_=x_v[G])
+
+        def load_qk(G):
+            a = pool.tile([P, PACK, 2, D], BF16, name="qk", tag="qk", bufs=1)
+            c = pool.tile([P, PACK, D // 2], BF16, name="cs", tag="cos", bufs=1)
+            s = pool.tile([P, PACK, D // 2], BF16, name="sn", tag="sin", bufs=1)
+            nc.sync.dma_start(out=a[:, :, 0, :], in_=qk_v[0][G])
+            nc.sync.dma_start(out=a[:, :, 1, :], in_=qk_v[1][G])
+            nc.sync.dma_start(out=c[:], in_=cos_v[G])
+            nc.sync.dma_start(out=s[:], in_=sin_v[G])
+            qkt[G] = (a, c, s)
+            if G == 0:
+                nc.sync.dma_start(out=sc_raw[:, 0, :], in_=q_scale.partition_broadcast(P))
+                nc.sync.dma_start(out=sc_raw[:, 1, :], in_=k_scale.partition_broadcast(P))
+
+        def rot(G):
+            if G == 0:
+                nc.vector.tensor_copy(
+                    out=sc[:].rearrange("p (t e i) -> p t e i", t=2, e=2), in_=sc_raw[:].rearrange("p t (i e) -> p t e i", e=2))
+            a, c, s = qkt[G]
+            p1 = pool.tile([P, PACK, 2, D], F32, name="p1", tag="p1", bufs=1)
+            p2 = pool.tile([P, PACK, 2, D], F32, name="p2", tag="p2", bufs=1)
+            b = pool.tile([P, PACK, D], F32, name="blk", tag="blk", bufs=1)
+            o = pool.tile([P, PACK, D], F32, name="gqk", tag="gqk", bufs=1)
+            gqk[G] = o
+            h = D // 2
+            shape = [P, PACK, 4, h]
+            av = a[:].rearrange("p j t (h i) -> p j (t h) i", h=2)
+            nc.vector.tensor_tensor(
+                out=p1[:].rearrange("p j t (h i) -> p j (t h) i", h=2), in0=av,
+                in1=c[:].unsqueeze(2).to_broadcast(shape), op=ALU.mult)
+            nc.vector.tensor_tensor(
+                out=p2[:].rearrange("p j t (h i) -> p j (t h) i", h=2), in0=av,
+                in1=s[:].unsqueeze(2).to_broadcast(shape), op=ALU.mult)
+            nc.vector.tensor_tensor(out=p1[:, :, :, :h], in0=p1[:, :, :, :h], in1=p2[:, :, :, h:], op=ALU.add)
+            nc.vector.tensor_tensor(out=p1[:, :, :, h:], in0=p1[:, :, :, h:], in1=p2[:, :, :, :h], op=ALU.subtract)
+            nc.vector.tensor_tensor(
+                out=p2[:].rearrange("p j t d -> p j (t d)"), in0=p1[:].rearrange("p j t d -> p j (t d)"),
+                in1=sc[:].unsqueeze(1).to_broadcast([P, PACK, 2 * D]), op=ALU.mult)
+            nc.vector.tensor_tensor(out=b[:], in0=p2[:, :, 0, :], in1=p2[:, :, 1, :], op=ALU.add)
+            nc.scalar.copy(
+                out=o[:].rearrange("p j (i e) -> p j i e", e=2), in_=b[:].rearrange("p j (e i) -> p j i e", e=2))
+
+        def sig(k, parts=1):
+            t = pool.tile([P, PACK, KP], F32, name="st", tag="s", bufs=2)
+            st[k] = t
+            w = KP // parts
+            for i in range(parts):
+                nc.scalar.activation(out=t[:, :, i * w : (i + 1) * w], in_=zt[k][:, :, i * w : (i + 1) * w], func=ACT.Sigmoid)
+
+        def mul_b(k, parts=1):
+            w = KP // parts
+            for i in range(parts):
+                c = slice(i * w, (i + 1) * w)
+                nc.vector.scalar_tensor_tensor(
+                    out=zt[k][:, :, c], in0=st[k][:, :, c], scalar=1.0, in1=zt[k][:, :, c], op0=ALU.subtract, op1=ALU.mult)
+
+        def mul_c(k):
+            nc.vector.scalar_tensor_tensor(out=st[k][:], in0=zt[k][:], scalar=1.0, in1=st[k][:], op0=ALU.subtract, op1=ALU.mult)
+
+        def segments(g):
+            lo, hi = g * KP, (g + 1) * KP
+            res = []
+            for a, b, w in ((0, E, 0), (E, 2 * E, 1), (2 * E, J, 2)):
+                x, y = max(lo, a), min(hi, b)
+                if x < y:
+                    res.append((x - lo, y - lo, w, x - a))
+            return res
+
+        def mul_d(k):
+            G, g = unit(k)
+            t = pool.tile([P, PACK * KP], BF16, name="dz", tag="dz", bufs=2, align_bytes=64)
+            dt_[k] = t
+            ov = t[:].rearrange("p (t q j) -> p q j t", t=PACK, j=PACK)
+            for a, b, w, off in segments(g):
+                src = gqk[G] if w == 2 else gt[w, G]
+                nc.vector.tensor_tensor(
+                    out=ov[:, a // 4 : b // 4, :, :],
+                    in0=st[k][:, :, a:b].rearrange("p j (q t) -> p q j t", t=PACK),
+                    in1=src[:, :, off : off + b - a].rearrange("p j (q t) -> p q j t", t=PACK),
+                    op=ALU.mult)
+
+        def quant_tok(k):
+            cod = pool.tile([P, KP], U32, name="tcod", tag="tcod%d" % (k // NF), bufs=NF if k < NF else 2, align_bytes=64)
+            scl = pool.tile([P, KP], U8, name="tscl", tag="tscl%d" % (k // NF), bufs=NF if k < NF else 2, align_bytes=64)
+            tcod[k], tscl[k] = cod, scl
+            nc.vector.quantize_mx(out=cod[:].bitcast(E5M2), scales=scl[:], in_=dt_[k][:])
+
+        def turn_dz(k, engines="ss"):
+            words = dt_[k][:].bitcast(F32)
+            f = pool.tile([P, PACK * KP], BF16, name="feat", tag="feat", bufs=4, align_bytes=64)
+            feat[k] = f
+            fv = f[:].rearrange("q (p j e t) -> q p j e t", j=2, e=2, t=PACK)
+            for jj in range(2):
+                bank = bank_of(jj, [P, PACK, P])
+                for t in range(PACK):
+                    nc.tensor.transpose(bank[:, t, :], words[:, 256 * t + jj : 256 * (t + 1) : 2], ident[:])
+                src = bank[:].bitcast(BF16).rearrange("q t (p e) -> q p e t", e=2)
+                if engines[jj] == "s":
+                    nc.scalar.copy(out=fv[:, :, jj, :, :], in_=src)
+                else:
+                    nc.vector.tensor_copy(out=fv[:, :, jj, :, :], in_=src)
+
+        def quant_feat(k):
+            G, g = unit(k)
+            nc.vector.quantize_mx(
+                out=f_codes[:, g, G * KP : (G + 1) * KP].bitcast(E5M2), scales=f_scales[:, g, G * KP : (G + 1) * KP], in_=feat[k][:])
+
+        def turn_w(a, g):
+            t, half = raw[a, g]
+            words = t[:].bitcast(F32)
+            f = pool.tile([P, PACK * KP], BF16, name="feat", tag="feat", bufs=4, align_bytes=64)
+            wfeat[a, g] = f
+            fw = f[:].bitcast(F32)
+            for hp in range(2):
+                bank = bank_of(2 + hp, [P, 2, 2, P])
+                for i in range(2):
+                    for u in range(2):
+                        nc.tensor.transpose(
+                            bank[:, u, i, :], words[:, 2 * hp + i, half * 256 + u : (half + 1) * 256 : 2], ident[:])
+                nc.scalar.copy(
+                    out=fw[:, hp * 512 : (hp + 1) * 512].rearrange("p (r u) -> p r u", u=2),
+                    in_=bank[:].rearrange("p u i r -> p (i r) u"))
+
+        def quant_w(a, g):
+            cols = slice(a * KP, (a + 1) * KP)
+            nc.vector.quantize_mx(out=w_codes[:, g, cols].bitcast(E4M3), scales=w_scales[:, g, cols], in_=wfeat[a, g][:])
+
+        def weave_x(G, half):
+            f = pool.tile([P, PACK * KP], BF16, name="feat", tag="feat", bufs=4, align_bytes=64)
+            xfeat[G, half] = f
+            nc.scalar.copy(
+                out=f[:].rearrange("p (w j) -> p w j", j=PACK),
+                in_=xraw[G][:, :, half * KP : (half + 1) * KP].rearrange("p j w -> p w j"))
+
+        def quant_x(G, half):
+            cols = slice(half * KP, (half + 1) * KP)
+            nc.vector.quantize_mx(out=x_codes[:, G, cols].bitcast(E4M3), scales=x_scales[:, G, cols], in_=xfeat[G, half][:])
+
+        def empty(eng, dst, src):
+            if eng == "s":
+                nc.scalar.activation(out=dst, in_=src, func=ACT.Copy, scale=-1.0)
+            else:
+                nc.vector.tensor_scalar(out=dst, in0=src, scalar1=-1.0, scalar2=None, op0=ALU.mult)
+
+        def prod0(G, hh, m, gs):
+            for g in gs:
+                if g == 0:
+                    acc0[G, hh, m] = bank_of(4 + m, [P, KP])
+                tok = slice(G * KP + m * P, G * KP + (m + 1) * P)
+                hs = slice(hh * KP, (hh + 1) * KP)
+                nc.tensor.matmul_mx(
+                    out=acc0[G, hh, m][:], lhsT=f_codes[:, g, tok].bitcast(E5M2), lhsT_scale=f_scales[:, g, tok],
+                    rhs=w_codes[:, g, hs].bitcast(E4M3), rhs_scale=w_scales[:, g, hs], start=(g == 0), stop=(g == NF - 1))
+
+        def store0(G, hh, m, eng):
+            o = pool.tile([P, KP], F32, name="o", tag="o", bufs=6)
+            empty(eng, o[:], acc0[G, hh, m][:])
+            nc.sync.dma_start(out=o0_v[4 * G + m, :, hh * KP : (hh + 1) * KP], in_=o[:])
+
+        def prod1(g, hb, eng):
+            bank = bank_of(2 + hb % 2, [P, KP])
+            hs = slice(hb * P, (hb + 1) * P)
+            for G in range(NG):
+                k = G * NF + g
+                nc.tensor.matmul_mx(
+                    out=bank[:], lhsT=x_codes[:, G, hs].bitcast(E4M3), lhsT_scale=x_scales[:, G, hs],
+                    rhs=tcod[k][:].bitcast(E5M2), rhs_scale=tscl[k][:], start=(G == 0), stop=(G == NG - 1))
+            o = pool.tile([P, KP], F32, name="o", tag="o", bufs=6)
+            empty(eng, o[:].rearrange("p (q t) -> p q t", t=PACK), bank[:].rearrange("p (t q) -> p q t", t=PACK))
+            nc.sync.dma_start(out=o1_v[hb, :, g * KP : (g + 1) * KP], in_=o[:])
+
+        ctx.enter_context(tc.manual_schedule())
+
+        nc.vector.memset(warm[:], 0.0)
+        nc.scalar.activation(out=warm[:], in_=warm[:], func=ACT.Sigmoid)
+        make_identity(nc, ident[:])
+        load_z(0, 2)
+        load_g(0, 0)
+        load_z(1)
+        load_w(0)
+        load_z(2)
+        load_w(1)
+        load_qk(0)
+        load_g(1, 0)
+        load_x(0)
+        sig(0, 2)
+
+        wsteps = [[(0, 0), (0, 1)], [(0, 2), (0, 3)], [(0, 4), (1, 0)], [(1, 1), (1, 2)], [(1, 3), (1, 4)]]
+        xsteps = {1: (0, 0), 2: (0, 1), 3: (1, 0), 4: (1, 1)}
+
+        for k in range(NF):
+            load_z(k + 3)
+            if k == 0:
+                load_w(2)
+            if k == 1:
+                load_g(0, 1)
+                load_w(3)
+            if k == 2:
+                load_x(1)
+                load_w(4)
+            if k == 3:
+                load_g(1, 1)
+                load_qk(1)
+            mul_b(k, 2 if k == 0 else 1)
+            if k > 0:
+                quant_tok(k - 1)
+            sig(k + 1)
+            for a, g in wsteps[k]:
+                turn_w(a, g)
+            mul_c(k)
+            if k > 0:
+                quant_feat(k - 1)
+                for m in range(4):
+                    prod0(0, 0, m, [k - 1])
+            if k in xsteps:
+                weave_x(*xsteps[k])
+            mul_d(k)
+            for a, g in wsteps[k]:
+                quant_w(a, g)
+            if k - 1 in xsteps:
+                quant_x(*xsteps[k - 1])
+            if k == 2:
+                rot(0)
+            turn_dz(k)
+
+        for k in range(NF, NU):
+            g = k - NF
+            if k + 3 < NU:
+                load_z(k + 3)
+            mul_b(k)
+            quant_tok(k - 1)
+            if k == NF:
+                sig(k + 1)
+                quant_x(*xsteps[4])
+            if g > 0:
+                for hb in range(4):
+                    prod1(g - 1, hb, "s")
+            if NF < k < NU - 1:
+                sig(k + 1)
+            mul_c(k)
+            quant_feat(k - 1)
+            if g == 0:
+                for m in range(4):
+                    prod0(0, 0, m, [NF - 1])
+                    store0(0, 0, m, "s")
+                for m in range(4):
+                    prod0(0, 1, m, range(NF))
+                    store0(0, 1, m, "s")
+            else:
+                for hb in range(4, 8):
+                    prod1(g - 1, hb, "s")
+                for m in range(4):
+                    prod0(1, 0, m, [g - 1])
+            mul_d(k)
+            if g == 2:
+                rot(1)
+            if k < NU - 1:
+                turn_dz(k)
+
+        quant_tok(NU - 1)
+        turn_dz(NU - 1, "sv")
+        for hb in range(4):
+            prod1(NF - 1, hb, "s")
+        quant_feat(NU - 1)
+        for m in range(4):
+            prod0(1, 0, m, [NF - 1])
+            store0(1, 0, m, "vsvs"[m])
+        for hb in range(4, 8):
+            prod1(NF - 1, hb, "vsvs"[hb - 4])
+        for m in range(4):
+            prod0(1, 1, m, range(NF))
+            store0(1, 1, m, "vsvs"[m])

@@ -3,7 +3,8 @@ from contextlib import ExitStack
 import concourse.mybir as mybir
 from concourse.masks import make_identity
 
-S, H, E, D = 1024, 1024, 1216, 128
+S, H = 1024, 1024
+E, D = 1216, 128
 J = 2 * E + D
 FLOPS = 2 * 2 * S * H * J
 
@@ -13,356 +14,362 @@ U32 = mybir.dt.uint32
 U8 = mybir.dt.uint8
 E4M3 = mybir.dt.float8_e4m3fn_x4
 E5M2 = mybir.dt.float8_e5m2_x4
-ALU = mybir.AluOpType
+ADD, SUB, MULT = mybir.AluOpType.add, mybir.AluOpType.subtract, mybir.AluOpType.mult
 ACT = mybir.ActivationFunctionType
 
 P = 128
 PACK = 4
-KP = P * PACK
-NG = S // KP
-NF = J // KP
+KG = P * PACK
+NG = S // KG
+NF = J // KG
 NU = NG * NF
+TILES = KG // P
+HALVES = H // KG
+WORK_BANKS = 8 - TILES
+HEAD_PARTS = 4
+HB = H // P
 
 
 def tile_gatedattentionunit_pa_v_kernel(
     tc, hidden_states, sin, cos, W_i, q_scale, k_scale, z, grad_0, grad_1, grad_2, grad_3, out_0, out_1
 ):
     nc = tc.nc
-    z_v = z.rearrange("b (g p j) w -> (b g) p j w", p=P, j=PACK)
-    x_v = hidden_states.rearrange("b (g p j) w -> (b g) p j w", p=P, j=PACK)
-    sin_v = sin.rearrange("b (g p j) w -> (b g) p j w", p=P, j=PACK)
-    cos_v = cos.rearrange("b (g p j) w -> (b g) p j w", p=P, j=PACK)
-    g_v = [t.rearrange("b (g p j) w -> (b g) p j w", p=P, j=PACK) for t in (grad_0, grad_1)]
-    qk_v = [t.rearrange("b (g p j) w -> (b g) p j w", p=P, j=PACK) for t in (grad_2, grad_3)]
-    w_v = W_i.rearrange("(a t p) k -> a p t k", p=P, t=4)
-    o0_v = out_0.rearrange("b (t p) h -> (b t) p h", p=P)
-    o1_v = out_1.rearrange("(t p) k -> t p k", p=P)
+
+    def by_token(t):
+        return t.rearrange("b (g p j) w -> (b g) p j w", p=P, j=PACK)
+
+    x_hbm, z_hbm, cos_hbm, sin_hbm = by_token(hidden_states), by_token(z), by_token(cos), by_token(sin)
+    grad_hbm = (by_token(grad_0), by_token(grad_1))
+    rot_hbm = (by_token(grad_2), by_token(grad_3))
+    w_hbm = W_i.rearrange("(a t p) k -> a p t k", p=P, t=TILES)
+    out_0_hbm = out_0.rearrange("b (t p) h -> (b t) p h", p=P)
+    out_1_hbm = out_1.rearrange("(t p) k -> t p k", p=P)
 
     with ExitStack() as ctx:
         keep = ctx.enter_context(tc.tile_pool(name="keep", bufs=1))
-        pool = ctx.enter_context(tc.tile_pool(name="pool", bufs=2))
-        psum = ctx.enter_context(tc.psum_pool(name="psum", bufs=2))
+        pool = ctx.enter_context(tc.tile_pool(name="pool", bufs=1))
+        psum = ctx.enter_context(tc.psum_pool(name="psum", bufs=1))
 
-        ident = keep.tile([P, P], F32, name="ident")
-        warm = keep.tile([P, 1], F32, name="warm")
         w_codes = keep.tile([P, NF, H], U32, name="w_codes", align_bytes=64)
         w_scales = keep.tile([P, NF, H], U8, name="w_scales", align_bytes=64)
         x_codes = keep.tile([P, NG, H], U32, name="x_codes", align_bytes=64)
         x_scales = keep.tile([P, NG, H], U8, name="x_scales", align_bytes=64)
         f_codes = keep.tile([P, NF, S], U32, name="f_codes", align_bytes=64)
         f_scales = keep.tile([P, NF, S], U8, name="f_scales", align_bytes=64)
-        sc_raw = keep.tile([P, 2, D], BF16, name="sc_raw")
-        sc = keep.tile([P, 2 * D], F32, name="sc")
+        ident = keep.tile([P, P], F32, name="ident")
+        ident_bf = keep.tile([P, P], BF16, name="ident_bf")
+        spread = keep.tile([P, P], F32, name="spread")
+        sign = keep.tile([P, 1], F32, name="sign")
+        gain_rows = keep.tile([P, 2, D], BF16, name="gain_rows")
+        gain_split = keep.tile([P, 2, D], BF16, name="gain_split")
+        gain = keep.tile([P, 2], F32, name="gain")
+        warm = keep.tile([P, 1], F32, name="warm")
 
-        zt, st, gt, dt_, raw, xraw, tcod, tscl, feat, gqk, qkt = {}, {}, {}, {}, {}, {}, {}, {}, {}, {}, {}
-        wfeat, xfeat, acc0 = {}, {}, {}
+        z_in, sig_out, grad_in, dz_out, t_codes, t_scales, f_in = {}, {}, {}, {}, {}, {}, {}
+        w_raw, w_in, x_raw, x_in, qk_in, rotated, gqk, sums = {}, {}, {}, {}, {}, {}, {}, {}
 
-        def bank_of(n, shape):
-            bank = psum.tile(shape, F32, name="bank", tag="b%d" % n, bufs=1)
+        work_turn = [0]
+
+        def work_bank(shape, dtype=F32):
+            work_turn[0] = (work_turn[0] + 1) % WORK_BANKS
+            bank = psum.tile(shape, dtype, name="work", tag="work%d" % work_turn[0])
             return bank
 
-        def unit(k):
-            return k // NF, k % NF
+        def quantise_input():
+            t = pool.tile([P, KG * PACK], BF16, name="q_in", tag="q_in", bufs=4, align_bytes=64)
+            return t
 
         def load_z(k, parts=1):
-            G, g = unit(k)
-            t = pool.tile([P, PACK, KP], F32, name="zt", tag="z", bufs=3)
-            zt[k] = t
-            w = KP // parts
+            z_in[k] = pool.tile([P, PACK, KG], F32, name="z_in", tag="z_in", bufs=3)
+            w, f0 = KG // parts, (k % NF) * KG
             for i in range(parts):
-                nc.sync.dma_start(out=t[:, :, i * w : (i + 1) * w], in_=z_v[G, :, :, g * KP + i * w : g * KP + (i + 1) * w])
+                nc.sync.dma_start(
+                    out=z_in[k][:, :, i * w : (i + 1) * w], in_=z_hbm[k // NF, :, :, f0 + i * w : f0 + (i + 1) * w])
 
-        def load_g(which, G):
-            t = pool.tile([P, PACK, E], BF16, name="gt", tag="g", bufs=3)
-            gt[which, G] = t
-            nc.sync.dma_start(out=t[:], in_=g_v[which][G])
+        def load_grad(which, G):
+            grad_in[which, G] = pool.tile([P, PACK, E], BF16, name="grad_in", tag="grad_in", bufs=3)
+            nc.sync.dma_start(out=grad_in[which, G][:], in_=grad_hbm[which][G])
 
-        w_order = [(0, 0), (0, 1), (0, 2), (0, 3), (0, 4), (1, 0), (1, 1), (1, 2), (1, 3), (1, 4)]
+        w_pieces = [(a, g) for a in range(HALVES) for g in range(NF)]
 
-        def load_w(s):
-            t = pool.tile([P, 4, 2 * KP], BF16, name="raw", tag="raw", bufs=3)
-            (a0, g0), (a1, g1) = w_order[2 * s], w_order[2 * s + 1]
+        def load_w(pair):
+            t = pool.tile([P, TILES, 2 * KG], BF16, name="raw", tag="raw", bufs=3)
+            (a0, g0), (a1, g1) = w_pieces[2 * pair], w_pieces[2 * pair + 1]
             if a0 == a1:
-                nc.sync.dma_start(out=t[:], in_=w_v[a0, :, :, g0 * KP : (g0 + 2) * KP])
+                nc.sync.dma_start(out=t[:], in_=w_hbm[a0, :, :, g0 * KG : (g1 + 1) * KG])
             else:
-                nc.sync.dma_start(out=t[:, :, :KP], in_=w_v[a0, :, :, g0 * KP : (g0 + 1) * KP])
-                nc.sync.dma_start(out=t[:, :, KP:], in_=w_v[a1, :, :, g1 * KP : (g1 + 1) * KP])
-            raw[a0, g0] = (t, 0)
-            raw[a1, g1] = (t, 1)
+                nc.sync.dma_start(out=t[:, :, :KG], in_=w_hbm[a0, :, :, g0 * KG : (g0 + 1) * KG])
+                nc.sync.dma_start(out=t[:, :, KG:], in_=w_hbm[a1, :, :, g1 * KG : (g1 + 1) * KG])
+            w_raw[a0, g0], w_raw[a1, g1] = (t, 0), (t, KG)
 
         def load_x(G):
-            t = pool.tile([P, PACK, H], BF16, name="raw", tag="raw", bufs=3)
-            xraw[G] = t
-            nc.sync.dma_start(out=t[:], in_=x_v[G])
+            x_raw[G] = pool.tile([P, PACK, H], BF16, name="raw", tag="raw", bufs=3)
+            nc.sync.dma_start(out=x_raw[G][:], in_=x_hbm[G])
 
-        def load_qk(G):
-            a = pool.tile([P, PACK, 2, D], BF16, name="qk", tag="qk", bufs=1)
-            c = pool.tile([P, PACK, D // 2], BF16, name="cs", tag="cos", bufs=1)
-            s = pool.tile([P, PACK, D // 2], BF16, name="sn", tag="sin", bufs=1)
-            nc.sync.dma_start(out=a[:, :, 0, :], in_=qk_v[0][G])
-            nc.sync.dma_start(out=a[:, :, 1, :], in_=qk_v[1][G])
-            nc.sync.dma_start(out=c[:], in_=cos_v[G])
-            nc.sync.dma_start(out=s[:], in_=sin_v[G])
-            qkt[G] = (a, c, s)
-            if G == 0:
-                nc.sync.dma_start(out=sc_raw[:, 0, :], in_=q_scale.partition_broadcast(P))
-                nc.sync.dma_start(out=sc_raw[:, 1, :], in_=k_scale.partition_broadcast(P))
+        def load_rotation(G):
+            qk = pool.tile([P, PACK, 2, D + D // 2], BF16, name="qk", tag="qk", bufs=1)
+            table = pool.tile([P, 2, PACK, D // 2], BF16, name="table", tag="table", bufs=1)
+            for i in range(2):
+                nc.sync.dma_start(out=qk[:, :, i, :D], in_=rot_hbm[i][G])
+                nc.sync.dma_start(out=table[:, i, :, :], in_=(cos_hbm, sin_hbm)[i][G])
+            qk_in[G] = (qk, table)
 
-        def rot(G):
-            if G == 0:
-                nc.vector.tensor_copy(
-                    out=sc[:].rearrange("p (t e i) -> p t e i", t=2, e=2), in_=sc_raw[:].rearrange("p t (i e) -> p t e i", e=2))
-            a, c, s = qkt[G]
-            p1 = pool.tile([P, PACK, 2, D], F32, name="p1", tag="p1", bufs=1)
-            p2 = pool.tile([P, PACK, 2, D], F32, name="p2", tag="p2", bufs=1)
-            b = pool.tile([P, PACK, D], F32, name="blk", tag="blk", bufs=1)
-            o = pool.tile([P, PACK, D], F32, name="gqk", tag="gqk", bufs=1)
-            gqk[G] = o
-            h = D // 2
-            shape = [P, PACK, 4, h]
-            av = a[:].rearrange("p j t (h i) -> p j (t h) i", h=2)
-            nc.vector.tensor_tensor(
-                out=p1[:].rearrange("p j t (h i) -> p j (t h) i", h=2), in0=av,
-                in1=c[:].unsqueeze(2).to_broadcast(shape), op=ALU.mult)
-            nc.vector.tensor_tensor(
-                out=p2[:].rearrange("p j t (h i) -> p j (t h) i", h=2), in0=av,
-                in1=s[:].unsqueeze(2).to_broadcast(shape), op=ALU.mult)
-            nc.vector.tensor_tensor(out=p1[:, :, :, :h], in0=p1[:, :, :, :h], in1=p2[:, :, :, h:], op=ALU.add)
-            nc.vector.tensor_tensor(out=p1[:, :, :, h:], in0=p1[:, :, :, h:], in1=p2[:, :, :, :h], op=ALU.subtract)
-            nc.vector.tensor_tensor(
-                out=p2[:].rearrange("p j t d -> p j (t d)"), in0=p1[:].rearrange("p j t d -> p j (t d)"),
-                in1=sc[:].unsqueeze(1).to_broadcast([P, PACK, 2 * D]), op=ALU.mult)
-            nc.vector.tensor_tensor(out=b[:], in0=p2[:, :, 0, :], in1=p2[:, :, 1, :], op=ALU.add)
-            nc.scalar.copy(
-                out=o[:].rearrange("p j (i e) -> p j i e", e=2), in_=b[:].rearrange("p j (e i) -> p j i e", e=2))
+        def load_gains():
+            nc.sync.dma_start(out=gain_rows[:, 0, :], in_=q_scale.partition_broadcast(P))
+            nc.sync.dma_start(out=gain_rows[:, 1, :], in_=k_scale.partition_broadcast(P))
 
-        def sig(k, parts=1):
-            t = pool.tile([P, PACK, KP], F32, name="st", tag="s", bufs=2)
-            st[k] = t
-            w = KP // parts
+        def prepare_rotation():
+            nc.vector.tensor_copy(out=ident_bf[:], in_=ident[:])
+            nc.vector.tensor_copy(
+                out=spread[:].rearrange("p (i e) -> p i e", e=2), in_=ident[:].rearrange("p (e i) -> p i e", e=2))
+            nc.vector.memset(sign[:], 1.0)
+            nc.vector.memset(sign[D // 2 :, :], -1.0)
+
+        def turn_gains():
+            nc.vector.tensor_copy(
+                out=gain_split[:].rearrange("p r (e i) -> p r e i", e=2),
+                in_=gain_rows[:].rearrange("p r (i e) -> p r e i", e=2))
+            bank = work_bank([P, 2, P], BF16)
+            for r in range(2):
+                nc.tensor.transpose(bank[:, r, :], gain_split[:, r, :], ident_bf[:])
+            nc.vector.tensor_copy(out=gain[:], in_=bank[:, :, 0])
+
+        def rotate(G):
+            qk, table = qk_in[G]
+            half = D // 2
+            twice = pool.tile([P, 2, PACK, 2, half], BF16, name="twice", tag="twice", bufs=1)
+            nc.vector.tensor_copy(out=qk[:, :, :, D:], in_=qk[:, :, :, :half])
+            nc.vector.tensor_copy(
+                out=twice[:].rearrange("p r j e i -> p (r j) e i"),
+                in_=table[:].rearrange("p r j i -> p (r j) i").unsqueeze(2).to_broadcast([P, 2 * PACK, 2, half]))
+            banks = []
+            for i in range(2):
+                bank = work_bank([P, 2, PACK, P], BF16)
+                for w in range(2):
+                    for j in range(PACK):
+                        nc.tensor.transpose(bank[:, w, j, :], qk[:, j, i, w * half : w * half + D], ident_bf[:])
+                banks.append(bank)
+            bank = work_bank([P, 2, PACK, P], BF16)
+            for r in range(2):
+                for j in range(PACK):
+                    nc.tensor.transpose(bank[:, r, j, :], twice[:, r, j, :, :].rearrange("p e i -> p (e i)"), ident_bf[:])
+            banks.append(bank)
+            q_road, k_road, trig = [bank[:].rearrange("c w j p -> c (w j p)") for bank in banks]
+            r = pool.tile([P, 2, KG], F32, name="rotated", tag="rotated", bufs=1)
+            rotated[G] = r
+            both = r[:].rearrange("p w n -> p (w n)")
+            nc.scalar.activation(out=both, in_=k_road, func=ACT.Copy, scale=gain[:, 1:2])
+            nc.vector.scalar_tensor_tensor(out=both, in0=q_road, scalar=gain[:, 0:1], in1=both, op0=MULT, op1=ADD)
+            nc.vector.tensor_tensor(out=both, in0=both, in1=trig, op=MULT)
+            nc.vector.scalar_tensor_tensor(
+                out=r[:, 0, :], in0=r[:, 1, :], scalar=sign[:], in1=r[:, 0, :], op0=MULT, op1=ADD)
+
+        def turn_back(G):
+            bank = work_bank([P, PACK, D])
+            for j in range(PACK):
+                nc.tensor.transpose(bank[:, j, :], rotated[G][:, 0, j * P : (j + 1) * P], spread[:])
+            gqk[G] = pool.tile([P, PACK, D], F32, name="gqk", tag="gqk", bufs=2)
+            nc.scalar.copy(out=gqk[G][:], in_=bank[:])
+
+        def sigmoid(k, parts=1):
+            sig_out[k] = pool.tile([P, PACK, KG], F32, name="sig_out", tag="sig_out", bufs=3)
+            w = KG // parts
             for i in range(parts):
-                nc.scalar.activation(out=t[:, :, i * w : (i + 1) * w], in_=zt[k][:, :, i * w : (i + 1) * w], func=ACT.Sigmoid)
+                cols = slice(i * w, (i + 1) * w)
+                nc.scalar.activation(out=sig_out[k][:, :, cols], in_=z_in[k][:, :, cols], func=ACT.Sigmoid)
 
-        def mul_b(k, parts=1):
-            w = KP // parts
+        def derivative_b(k, parts=1):
+            w = KG // parts
             for i in range(parts):
-                c = slice(i * w, (i + 1) * w)
-                nc.vector.scalar_tensor_tensor(
-                    out=zt[k][:, :, c], in0=st[k][:, :, c], scalar=1.0, in1=zt[k][:, :, c], op0=ALU.subtract, op1=ALU.mult)
+                zc, sc = z_in[k][:, :, i * w : (i + 1) * w], sig_out[k][:, :, i * w : (i + 1) * w]
+                nc.vector.scalar_tensor_tensor(out=zc, in0=sc, scalar=1.0, in1=zc, op0=SUB, op1=MULT)
 
-        def mul_c(k):
-            nc.vector.scalar_tensor_tensor(out=st[k][:], in0=zt[k][:], scalar=1.0, in1=st[k][:], op0=ALU.subtract, op1=ALU.mult)
+        def derivative_c(k):
+            nc.vector.scalar_tensor_tensor(
+                out=sig_out[k][:], in0=z_in[k][:], scalar=1.0, in1=sig_out[k][:], op0=SUB, op1=MULT)
 
-        def segments(g):
-            lo, hi = g * KP, (g + 1) * KP
-            res = []
-            for a, b, w in ((0, E, 0), (E, 2 * E, 1), (2 * E, J, 2)):
-                x, y = max(lo, a), min(hi, b)
-                if x < y:
-                    res.append((x - lo, y - lo, w, x - a))
-            return res
+        def times_grad(k):
+            G, f0 = k // NF, (k % NF) * KG
+            dz_out[k] = pool.tile([P, PACK * KG], BF16, name="dz_out", tag="dz_out", bufs=2, align_bytes=64)
+            out = dz_out[k][:].rearrange("p (t q j) -> p q t j", t=PACK, j=PACK)
+            for first, last, src in ((0, E, 0), (E, 2 * E, 1), (2 * E, J, 2)):
+                lo, hi = max(f0, first), min(f0 + KG, last)
+                if lo < hi:
+                    grad = gqk[G] if src == 2 else grad_in[src, G]
+                    nc.vector.tensor_tensor(
+                        out=out[:, (lo - f0) // PACK : (hi - f0) // PACK, :, :],
+                        in0=sig_out[k][:, :, lo - f0 : hi - f0].rearrange("p j (q t) -> p q t j", t=PACK),
+                        in1=grad[:, :, lo - first : hi - first].rearrange("p j (q t) -> p q t j", t=PACK),
+                        op=MULT)
 
-        def mul_d(k):
-            G, g = unit(k)
-            t = pool.tile([P, PACK * KP], BF16, name="dz", tag="dz", bufs=2, align_bytes=64)
-            dt_[k] = t
-            ov = t[:].rearrange("p (t q j) -> p q j t", t=PACK, j=PACK)
-            for a, b, w, off in segments(g):
-                src = gqk[G] if w == 2 else gt[w, G]
-                nc.vector.tensor_tensor(
-                    out=ov[:, a // 4 : b // 4, :, :],
-                    in0=st[k][:, :, a:b].rearrange("p j (q t) -> p q j t", t=PACK),
-                    in1=src[:, :, off : off + b - a].rearrange("p j (q t) -> p q j t", t=PACK),
-                    op=ALU.mult)
+        def quantise_tokens(k):
+            t_codes[k] = pool.tile([P, KG], U32, name="t_codes", tag="t_codes", bufs=7, align_bytes=64)
+            t_scales[k] = pool.tile([P, KG], U8, name="t_scales", tag="t_scales", bufs=7, align_bytes=64)
+            nc.vector.quantize_mx(out=t_codes[k][:].bitcast(E5M2), scales=t_scales[k][:], in_=dz_out[k][:])
 
-        def quant_tok(k):
-            cod = pool.tile([P, KP], U32, name="tcod", tag="tcod%d" % (k // NF), bufs=NF if k < NF else 2, align_bytes=64)
-            scl = pool.tile([P, KP], U8, name="tscl", tag="tscl%d" % (k // NF), bufs=NF if k < NF else 2, align_bytes=64)
-            tcod[k], tscl[k] = cod, scl
-            nc.vector.quantize_mx(out=cod[:].bitcast(E5M2), scales=scl[:], in_=dt_[k][:])
-
-        def turn_dz(k, engines="ss"):
-            words = dt_[k][:].bitcast(F32)
-            f = pool.tile([P, PACK * KP], BF16, name="feat", tag="feat", bufs=4, align_bytes=64)
-            feat[k] = f
-            fv = f[:].rearrange("q (p j e t) -> q p j e t", j=2, e=2, t=PACK)
-            for jj in range(2):
-                bank = bank_of(jj, [P, PACK, P])
+        def turn_dz(k, copies):
+            words = dz_out[k][:].bitcast(F32)
+            f_in[k] = quantise_input()
+            out = f_in[k][:].rearrange("q (p u e t) -> q p u e t", u=2, e=2, t=PACK)
+            for u in range(2):
+                bank = work_bank([P, PACK, P])
                 for t in range(PACK):
-                    nc.tensor.transpose(bank[:, t, :], words[:, 256 * t + jj : 256 * (t + 1) : 2], ident[:])
-                src = bank[:].bitcast(BF16).rearrange("q t (p e) -> q p e t", e=2)
-                if engines[jj] == "s":
-                    nc.scalar.copy(out=fv[:, :, jj, :, :], in_=src)
-                else:
-                    nc.vector.tensor_copy(out=fv[:, :, jj, :, :], in_=src)
+                    nc.tensor.transpose(bank[:, t, :], words[:, 2 * P * t + u : 2 * P * (t + 1) : 2], ident[:])
+                copies[u](out=out[:, :, u, :, :], in_=bank[:].bitcast(BF16).rearrange("q t (p e) -> q p e t", e=2))
 
-        def quant_feat(k):
-            G, g = unit(k)
+        def quantise_features(k):
+            cols = slice(k // NF * KG, (k // NF + 1) * KG)
             nc.vector.quantize_mx(
-                out=f_codes[:, g, G * KP : (G + 1) * KP].bitcast(E5M2), scales=f_scales[:, g, G * KP : (G + 1) * KP], in_=feat[k][:])
+                out=f_codes[:, k % NF, cols].bitcast(E5M2), scales=f_scales[:, k % NF, cols], in_=f_in[k][:])
 
         def turn_w(a, g):
-            t, half = raw[a, g]
-            words = t[:].bitcast(F32)
-            f = pool.tile([P, PACK * KP], BF16, name="feat", tag="feat", bufs=4, align_bytes=64)
-            wfeat[a, g] = f
-            fw = f[:].bitcast(F32)
-            for hp in range(2):
-                bank = bank_of(2 + hp, [P, 2, 2, P])
+            raw, off = w_raw[a, g]
+            words = raw[:].bitcast(F32)
+            w_in[a, g] = quantise_input()
+            out = w_in[a, g][:].bitcast(F32)
+            for pair in range(TILES // 2):
+                bank = work_bank([P, 2, 2, P])
                 for i in range(2):
                     for u in range(2):
                         nc.tensor.transpose(
-                            bank[:, u, i, :], words[:, 2 * hp + i, half * 256 + u : (half + 1) * 256 : 2], ident[:])
+                            bank[:, u, i, :], words[:, 2 * pair + i, off // 2 + u : (off + KG) // 2 : 2], ident[:])
                 nc.scalar.copy(
-                    out=fw[:, hp * 512 : (hp + 1) * 512].rearrange("p (r u) -> p r u", u=2),
-                    in_=bank[:].rearrange("p u i r -> p (i r) u"))
+                    out=out[:, pair * KG : (pair + 1) * KG].rearrange("q (r u) -> q r u", u=2),
+                    in_=bank[:].rearrange("q u i r -> q (i r) u"))
 
-        def quant_w(a, g):
-            cols = slice(a * KP, (a + 1) * KP)
-            nc.vector.quantize_mx(out=w_codes[:, g, cols].bitcast(E4M3), scales=w_scales[:, g, cols], in_=wfeat[a, g][:])
+        def quantise_w(a, g):
+            cols = slice(a * KG, (a + 1) * KG)
+            nc.vector.quantize_mx(out=w_codes[:, g, cols].bitcast(E4M3), scales=w_scales[:, g, cols], in_=w_in[a, g][:])
 
-        def weave_x(G, half):
-            f = pool.tile([P, PACK * KP], BF16, name="feat", tag="feat", bufs=4, align_bytes=64)
-            xfeat[G, half] = f
+        def weave_x(G, a):
+            x_in[G, a] = quantise_input()
             nc.scalar.copy(
-                out=f[:].rearrange("p (w j) -> p w j", j=PACK),
-                in_=xraw[G][:, :, half * KP : (half + 1) * KP].rearrange("p j w -> p w j"))
+                out=x_in[G, a][:].rearrange("p (w j) -> p w j", j=PACK),
+                in_=x_raw[G][:, :, a * KG : (a + 1) * KG].rearrange("p j w -> p w j"))
 
-        def quant_x(G, half):
-            cols = slice(half * KP, (half + 1) * KP)
-            nc.vector.quantize_mx(out=x_codes[:, G, cols].bitcast(E4M3), scales=x_scales[:, G, cols], in_=xfeat[G, half][:])
+        def quantise_x(G, a):
+            cols = slice(a * KG, (a + 1) * KG)
+            nc.vector.quantize_mx(out=x_codes[:, G, cols].bitcast(E4M3), scales=x_scales[:, G, cols], in_=x_in[G, a][:])
 
-        def empty(eng, dst, src):
-            if eng == "s":
-                nc.scalar.activation(out=dst, in_=src, func=ACT.Copy, scale=-1.0)
-            else:
-                nc.vector.tensor_scalar(out=dst, in0=src, scalar1=-1.0, scalar2=None, op0=ALU.mult)
+        def negate_scalar(out, in_):
+            nc.scalar.activation(out=out, in_=in_, func=ACT.Copy, scale=-1.0)
 
-        def prod0(G, hh, m, gs):
-            for g in gs:
-                if g == 0:
-                    acc0[G, hh, m] = bank_of(4 + m, [P, KP])
-                tok = slice(G * KP + m * P, G * KP + (m + 1) * P)
-                hs = slice(hh * KP, (hh + 1) * KP)
-                nc.tensor.matmul_mx(
-                    out=acc0[G, hh, m][:], lhsT=f_codes[:, g, tok].bitcast(E5M2), lhsT_scale=f_scales[:, g, tok],
-                    rhs=w_codes[:, g, hs].bitcast(E4M3), rhs_scale=w_scales[:, g, hs], start=(g == 0), stop=(g == NF - 1))
+        def negate_vector(out, in_):
+            nc.vector.tensor_scalar(out=out, in0=in_, scalar1=-1.0, scalar2=None, op0=MULT)
 
-        def store0(G, hh, m, eng):
-            o = pool.tile([P, KP], F32, name="o", tag="o", bufs=6)
-            empty(eng, o[:], acc0[G, hh, m][:])
-            nc.sync.dma_start(out=o0_v[4 * G + m, :, hh * KP : (hh + 1) * KP], in_=o[:])
+        def result_tile():
+            t = pool.tile([P, KG], F32, name="result", tag="result", bufs=9)
+            return t
 
-        def prod1(g, hb, eng):
-            bank = bank_of(2 + hb % 2, [P, KP])
-            hs = slice(hb * P, (hb + 1) * P)
+        def add_out_0(G, a, groups, empty):
+            cols = slice(a * KG, (a + 1) * KG)
+            for m in range(TILES):
+                rows = slice(G * KG + m * P, G * KG + (m + 1) * P)
+                for g in groups:
+                    if g == 0:
+                        sums[G, a, m] = psum.tile([P, KG], F32, name="sums", tag="sums%d" % m)
+                    nc.tensor.matmul_mx(
+                        out=sums[G, a, m][:],
+                        lhsT=f_codes[:, g, rows].bitcast(E5M2), lhsT_scale=f_scales[:, g, rows],
+                        rhs=w_codes[:, g, cols].bitcast(E4M3), rhs_scale=w_scales[:, g, cols],
+                        start=(g == 0), stop=(g == NF - 1))
+                if NF - 1 in groups:
+                    result = result_tile()
+                    empty[m](result[:], sums[G, a, m][:])
+                    nc.sync.dma_start(out=out_0_hbm[TILES * G + m, :, cols], in_=result[:])
+
+        def make_out_1(g, hb, empty):
+            bank = work_bank([P, KG])
+            rows = slice(hb * P, (hb + 1) * P)
             for G in range(NG):
                 k = G * NF + g
                 nc.tensor.matmul_mx(
-                    out=bank[:], lhsT=x_codes[:, G, hs].bitcast(E4M3), lhsT_scale=x_scales[:, G, hs],
-                    rhs=tcod[k][:].bitcast(E5M2), rhs_scale=tscl[k][:], start=(G == 0), stop=(G == NG - 1))
-            o = pool.tile([P, KP], F32, name="o", tag="o", bufs=6)
-            empty(eng, o[:].rearrange("p (q t) -> p q t", t=PACK), bank[:].rearrange("p (t q) -> p q t", t=PACK))
-            nc.sync.dma_start(out=o1_v[hb, :, g * KP : (g + 1) * KP], in_=o[:])
+                    out=bank[:],
+                    lhsT=x_codes[:, G, rows].bitcast(E4M3), lhsT_scale=x_scales[:, G, rows],
+                    rhs=t_codes[k][:].bitcast(E5M2), rhs_scale=t_scales[k][:],
+                    start=(G == 0), stop=(G == NG - 1))
+            result = result_tile()
+            empty(result[:].rearrange("p (q t) -> p q t", t=PACK), bank[:].rearrange("p (t q) -> p q t", t=PACK))
+            nc.sync.dma_start(out=out_1_hbm[hb, :, g * KG : (g + 1) * KG], in_=result[:])
 
-        ctx.enter_context(tc.manual_schedule())
+        scalar_four, both_four = [negate_scalar] * TILES, [negate_vector, negate_scalar] * (TILES // 2)
 
         nc.vector.memset(warm[:], 0.0)
         nc.scalar.activation(out=warm[:], in_=warm[:], func=ACT.Sigmoid)
         make_identity(nc, ident[:])
-        load_z(0, 2)
-        load_g(0, 0)
+        load_z(0, HEAD_PARTS)
+        load_grad(0, 0)
         load_z(1)
         load_w(0)
         load_z(2)
         load_w(1)
-        load_qk(0)
-        load_g(1, 0)
+        load_rotation(0)
+        load_gains()
+        load_grad(1, 0)
         load_x(0)
-        sig(0, 2)
+        load_x(1)
+        sigmoid(0, HEAD_PARTS)
+        sigmoid(1)
+        prepare_rotation()
 
-        wsteps = [[(0, 0), (0, 1)], [(0, 2), (0, 3)], [(0, 4), (1, 0)], [(1, 1), (1, 2)], [(1, 3), (1, 4)]]
-        xsteps = {1: (0, 0), 2: (0, 1), 3: (1, 0), 4: (1, 1)}
-
-        for k in range(NF):
-            load_z(k + 3)
-            if k == 0:
-                load_w(2)
-            if k == 1:
-                load_g(0, 1)
-                load_w(3)
-            if k == 2:
-                load_x(1)
-                load_w(4)
-            if k == 3:
-                load_g(1, 1)
-                load_qk(1)
-            mul_b(k, 2 if k == 0 else 1)
+        x_pieces = [(G, a) for G in range(NG) for a in range(HALVES)]
+        quantised = turned = 0
+        for k in range(NU):
+            if k < 2:
+                load_grad(k, 1)
+            if 1 <= k <= 3:
+                load_w(k + 1)
+            derivative_b(k, HEAD_PARTS if k == 0 else 1)
             if k > 0:
-                quant_tok(k - 1)
-            sig(k + 1)
-            for a, g in wsteps[k]:
-                turn_w(a, g)
-            mul_c(k)
-            if k > 0:
-                quant_feat(k - 1)
-                for m in range(4):
-                    prod0(0, 0, m, [k - 1])
-            if k in xsteps:
-                weave_x(*xsteps[k])
-            mul_d(k)
-            for a, g in wsteps[k]:
-                quant_w(a, g)
-            if k - 1 in xsteps:
-                quant_x(*xsteps[k - 1])
-            if k == 2:
-                rot(0)
-            turn_dz(k)
-
-        for k in range(NF, NU):
-            g = k - NF
+                quantise_tokens(k - 1)
+                for piece in w_pieces[quantised:turned]:
+                    quantise_w(*piece)
+                if k + 1 < NU:
+                    sigmoid(k + 1)
+            quantised = turned
+            if 2 <= k <= len(x_pieces) + 1:
+                quantise_x(*x_pieces[k - 2])
+            turned = min(len(w_pieces), max(k + 1, 2 * k))
+            for piece in w_pieces[quantised:turned]:
+                turn_w(*piece)
+            if k > NF:
+                for hb in range(HB // 2):
+                    make_out_1(k - NF - 1, hb, negate_scalar)
+            derivative_c(k)
             if k + 3 < NU:
                 load_z(k + 3)
-            mul_b(k)
-            quant_tok(k - 1)
-            if k == NF:
-                sig(k + 1)
-                quant_x(*xsteps[4])
-            if g > 0:
-                for hb in range(4):
-                    prod1(g - 1, hb, "s")
-            if NF < k < NU - 1:
-                sig(k + 1)
-            mul_c(k)
-            quant_feat(k - 1)
-            if g == 0:
-                for m in range(4):
-                    prod0(0, 0, m, [NF - 1])
-                    store0(0, 0, m, "s")
-                for m in range(4):
-                    prod0(0, 1, m, range(NF))
-                    store0(0, 1, m, "s")
-            else:
-                for hb in range(4, 8):
-                    prod1(g - 1, hb, "s")
-                for m in range(4):
-                    prod0(1, 0, m, [g - 1])
-            mul_d(k)
-            if g == 2:
-                rot(1)
+            if k > 0:
+                quantise_features(k - 1)
+            if k > NF:
+                for hb in range(HB // 2, HB):
+                    make_out_1(k - NF - 1, hb, negate_scalar)
+            if 1 <= k <= NF:
+                add_out_0(0, 0, [k - 1], scalar_four)
+            if k == NF + 1:
+                add_out_0(0, 1, range(NF), scalar_four)
+            if k == NF + 2:
+                add_out_0(1, 0, range(2), scalar_four)
+            if k > NF + 2:
+                add_out_0(1, 0, [k - NF - 1], scalar_four)
+            if 1 <= k <= len(x_pieces):
+                weave_x(*x_pieces[k - 1])
+            times_grad(k)
             if k < NU - 1:
-                turn_dz(k)
+                turn_dz(k, (nc.scalar.copy, nc.scalar.copy))
+            if k == 2:
+                turn_gains()
+                rotate(0)
+                load_rotation(1)
+            if k == 3:
+                turn_back(0)
+                rotate(1)
+            if k == 4:
+                turn_back(1)
 
-        quant_tok(NU - 1)
-        turn_dz(NU - 1, "sv")
-        for hb in range(4):
-            prod1(NF - 1, hb, "s")
-        quant_feat(NU - 1)
-        for m in range(4):
-            prod0(1, 0, m, [NF - 1])
-            store0(1, 0, m, "vsvs"[m])
-        for hb in range(4, 8):
-            prod1(NF - 1, hb, "vsvs"[hb - 4])
-        for m in range(4):
-            prod0(1, 1, m, range(NF))
-            store0(1, 1, m, "vsvs"[m])
+        quantise_tokens(NU - 1)
+        turn_dz(NU - 1, (nc.scalar.copy, nc.vector.tensor_copy))
+        quantise_features(NU - 1)
+        add_out_0(1, 0, [NF - 1], both_four)
+        for hb in range(HB):
+            make_out_1(NF - 1, hb, (negate_vector, negate_scalar)[hb % 2])
+        add_out_0(1, 1, range(NF), both_four)

from contextlib import ExitStack

import concourse.mybir as mybir
from concourse.masks import make_identity

S, H = 1024, 1024
E, D = 1216, 128
J = 2 * E + D
FLOPS = 2 * 2 * S * H * J

F32 = mybir.dt.float32
BF16 = mybir.dt.bfloat16
U32 = mybir.dt.uint32
U8 = mybir.dt.uint8
E4M3 = mybir.dt.float8_e4m3fn_x4
E5M2 = mybir.dt.float8_e5m2_x4
ADD, SUB, MULT = mybir.AluOpType.add, mybir.AluOpType.subtract, mybir.AluOpType.mult
ACT = mybir.ActivationFunctionType

P = 128
PACK = 4
KG = P * PACK
NG = S // KG
NF = J // KG
NU = NG * NF
TILES = KG // P
HALVES = H // KG
WORK_BANKS = 8 - TILES
HEAD_PARTS = 4
HB = H // P


def tile_gatedattentionunit_pa_v_kernel(
    tc, hidden_states, sin, cos, W_i, q_scale, k_scale, z, grad_0, grad_1, grad_2, grad_3, out_0, out_1
):
    nc = tc.nc

    def by_token(t):
        return t.rearrange("b (g p j) w -> (b g) p j w", p=P, j=PACK)

    x_hbm, z_hbm, cos_hbm, sin_hbm = by_token(hidden_states), by_token(z), by_token(cos), by_token(sin)
    grad_hbm = (by_token(grad_0), by_token(grad_1))
    rot_hbm = (by_token(grad_2), by_token(grad_3))
    w_hbm = W_i.rearrange("(a t p) k -> a p t k", p=P, t=TILES)
    out_0_hbm = out_0.rearrange("b (t p) h -> (b t) p h", p=P)
    out_1_hbm = out_1.rearrange("(t p) k -> t p k", p=P)

    with ExitStack() as ctx:
        keep = ctx.enter_context(tc.tile_pool(name="keep", bufs=1))
        pool = ctx.enter_context(tc.tile_pool(name="pool", bufs=1))
        psum = ctx.enter_context(tc.psum_pool(name="psum", bufs=1))

        w_codes = keep.tile([P, NF, H], U32, name="w_codes", align_bytes=64)
        w_scales = keep.tile([P, NF, H], U8, name="w_scales", align_bytes=64)
        x_codes = keep.tile([P, NG, H], U32, name="x_codes", align_bytes=64)
        x_scales = keep.tile([P, NG, H], U8, name="x_scales", align_bytes=64)
        f_codes = keep.tile([P, NF, S], U32, name="f_codes", align_bytes=64)
        f_scales = keep.tile([P, NF, S], U8, name="f_scales", align_bytes=64)
        ident = keep.tile([P, P], F32, name="ident")
        ident_bf = keep.tile([P, P], BF16, name="ident_bf")
        spread = keep.tile([P, P], F32, name="spread")
        sign = keep.tile([P, 1], F32, name="sign")
        gain_rows = keep.tile([P, 2, D], BF16, name="gain_rows")
        gain_split = keep.tile([P, 2, D], BF16, name="gain_split")
        gain = keep.tile([P, 2], F32, name="gain")
        warm = keep.tile([P, 1], F32, name="warm")

        z_in, sig_out, grad_in, dz_out, t_codes, t_scales, f_in = {}, {}, {}, {}, {}, {}, {}
        w_raw, w_in, x_raw, x_in, qk_in, rotated, gqk, sums = {}, {}, {}, {}, {}, {}, {}, {}

        work_turn = [0]

        def work_bank(shape, dtype=F32):
            work_turn[0] = (work_turn[0] + 1) % WORK_BANKS
            bank = psum.tile(shape, dtype, name="work", tag="work%d" % work_turn[0])
            return bank

        def quantise_input():
            t = pool.tile([P, KG * PACK], BF16, name="q_in", tag="q_in", bufs=4, align_bytes=64)
            return t

        def load_z(k, parts=1):
            z_in[k] = pool.tile([P, PACK, KG], F32, name="z_in", tag="z_in", bufs=3)
            w, f0 = KG // parts, (k % NF) * KG
            for i in range(parts):
                nc.sync.dma_start(
                    out=z_in[k][:, :, i * w : (i + 1) * w], in_=z_hbm[k // NF, :, :, f0 + i * w : f0 + (i + 1) * w])

        def load_grad(which, G):
            grad_in[which, G] = pool.tile([P, PACK, E], BF16, name="grad_in", tag="grad_in", bufs=3)
            nc.sync.dma_start(out=grad_in[which, G][:], in_=grad_hbm[which][G])

        w_pieces = [(a, g) for a in range(HALVES) for g in range(NF)]

        def load_w(pair):
            t = pool.tile([P, TILES, 2 * KG], BF16, name="raw", tag="raw", bufs=3)
            (a0, g0), (a1, g1) = w_pieces[2 * pair], w_pieces[2 * pair + 1]
            if a0 == a1:
                nc.sync.dma_start(out=t[:], in_=w_hbm[a0, :, :, g0 * KG : (g1 + 1) * KG])
            else:
                nc.sync.dma_start(out=t[:, :, :KG], in_=w_hbm[a0, :, :, g0 * KG : (g0 + 1) * KG])
                nc.sync.dma_start(out=t[:, :, KG:], in_=w_hbm[a1, :, :, g1 * KG : (g1 + 1) * KG])
            w_raw[a0, g0], w_raw[a1, g1] = (t, 0), (t, KG)

        def load_x(G):
            x_raw[G] = pool.tile([P, PACK, H], BF16, name="raw", tag="raw", bufs=3)
            nc.sync.dma_start(out=x_raw[G][:], in_=x_hbm[G])

        def load_rotation(G):
            qk = pool.tile([P, PACK, 2, D + D // 2], BF16, name="qk", tag="qk", bufs=1)
            table = pool.tile([P, 2, PACK, D // 2], BF16, name="table", tag="table", bufs=1)
            for i in range(2):
                nc.sync.dma_start(out=qk[:, :, i, :D], in_=rot_hbm[i][G])
                nc.sync.dma_start(out=table[:, i, :, :], in_=(cos_hbm, sin_hbm)[i][G])
            qk_in[G] = (qk, table)

        def load_gains():
            nc.sync.dma_start(out=gain_rows[:, 0, :], in_=q_scale.partition_broadcast(P))
            nc.sync.dma_start(out=gain_rows[:, 1, :], in_=k_scale.partition_broadcast(P))

        def prepare_rotation():
            nc.vector.tensor_copy(out=ident_bf[:], in_=ident[:])
            nc.vector.tensor_copy(
                out=spread[:].rearrange("p (i e) -> p i e", e=2), in_=ident[:].rearrange("p (e i) -> p i e", e=2))
            nc.vector.memset(sign[:], 1.0)
            nc.vector.memset(sign[D // 2 :, :], -1.0)

        def turn_gains():
            nc.vector.tensor_copy(
                out=gain_split[:].rearrange("p r (e i) -> p r e i", e=2),
                in_=gain_rows[:].rearrange("p r (i e) -> p r e i", e=2))
            bank = work_bank([P, 2, P], BF16)
            for r in range(2):
                nc.tensor.transpose(bank[:, r, :], gain_split[:, r, :], ident_bf[:])
            nc.vector.tensor_copy(out=gain[:], in_=bank[:, :, 0])

        def rotate(G):
            qk, table = qk_in[G]
            half = D // 2
            twice = pool.tile([P, 2, PACK, 2, half], BF16, name="twice", tag="twice", bufs=1)
            nc.vector.tensor_copy(out=qk[:, :, :, D:], in_=qk[:, :, :, :half])
            nc.vector.tensor_copy(
                out=twice[:].rearrange("p r j e i -> p (r j) e i"),
                in_=table[:].rearrange("p r j i -> p (r j) i").unsqueeze(2).to_broadcast([P, 2 * PACK, 2, half]))
            banks = []
            for i in range(2):
                bank = work_bank([P, 2, PACK, P], BF16)
                for w in range(2):
                    for j in range(PACK):
                        nc.tensor.transpose(bank[:, w, j, :], qk[:, j, i, w * half : w * half + D], ident_bf[:])
                banks.append(bank)
            bank = work_bank([P, 2, PACK, P], BF16)
            for r in range(2):
                for j in range(PACK):
                    nc.tensor.transpose(bank[:, r, j, :], twice[:, r, j, :, :].rearrange("p e i -> p (e i)"), ident_bf[:])
            banks.append(bank)
            q_road, k_road, trig = [bank[:].rearrange("c w j p -> c (w j p)") for bank in banks]
            r = pool.tile([P, 2, KG], F32, name="rotated", tag="rotated", bufs=1)
            rotated[G] = r
            both = r[:].rearrange("p w n -> p (w n)")
            nc.scalar.activation(out=both, in_=k_road, func=ACT.Copy, scale=gain[:, 1:2])
            nc.vector.scalar_tensor_tensor(out=both, in0=q_road, scalar=gain[:, 0:1], in1=both, op0=MULT, op1=ADD)
            nc.vector.tensor_tensor(out=both, in0=both, in1=trig, op=MULT)
            nc.vector.scalar_tensor_tensor(
                out=r[:, 0, :], in0=r[:, 1, :], scalar=sign[:], in1=r[:, 0, :], op0=MULT, op1=ADD)

        def turn_back(G):
            bank = work_bank([P, PACK, D])
            for j in range(PACK):
                nc.tensor.transpose(bank[:, j, :], rotated[G][:, 0, j * P : (j + 1) * P], spread[:])
            gqk[G] = pool.tile([P, PACK, D], F32, name="gqk", tag="gqk", bufs=2)
            nc.scalar.copy(out=gqk[G][:], in_=bank[:])

        def sigmoid(k, parts=1):
            sig_out[k] = pool.tile([P, PACK, KG], F32, name="sig_out", tag="sig_out", bufs=3)
            w = KG // parts
            for i in range(parts):
                cols = slice(i * w, (i + 1) * w)
                nc.scalar.activation(out=sig_out[k][:, :, cols], in_=z_in[k][:, :, cols], func=ACT.Sigmoid)

        def derivative_b(k, parts=1):
            w = KG // parts
            for i in range(parts):
                zc, sc = z_in[k][:, :, i * w : (i + 1) * w], sig_out[k][:, :, i * w : (i + 1) * w]
                nc.vector.scalar_tensor_tensor(out=zc, in0=sc, scalar=1.0, in1=zc, op0=SUB, op1=MULT)

        def derivative_c(k):
            nc.vector.scalar_tensor_tensor(
                out=sig_out[k][:], in0=z_in[k][:], scalar=1.0, in1=sig_out[k][:], op0=SUB, op1=MULT)

        def times_grad(k):
            G, f0 = k // NF, (k % NF) * KG
            dz_out[k] = pool.tile([P, PACK * KG], BF16, name="dz_out", tag="dz_out", bufs=2, align_bytes=64)
            out = dz_out[k][:].rearrange("p (t q j) -> p q t j", t=PACK, j=PACK)
            for first, last, src in ((0, E, 0), (E, 2 * E, 1), (2 * E, J, 2)):
                lo, hi = max(f0, first), min(f0 + KG, last)
                if lo < hi:
                    grad = gqk[G] if src == 2 else grad_in[src, G]
                    nc.vector.tensor_tensor(
                        out=out[:, (lo - f0) // PACK : (hi - f0) // PACK, :, :],
                        in0=sig_out[k][:, :, lo - f0 : hi - f0].rearrange("p j (q t) -> p q t j", t=PACK),
                        in1=grad[:, :, lo - first : hi - first].rearrange("p j (q t) -> p q t j", t=PACK),
                        op=MULT)

        def quantise_tokens(k):
            t_codes[k] = pool.tile([P, KG], U32, name="t_codes", tag="t_codes", bufs=7, align_bytes=64)
            t_scales[k] = pool.tile([P, KG], U8, name="t_scales", tag="t_scales", bufs=7, align_bytes=64)
            nc.vector.quantize_mx(out=t_codes[k][:].bitcast(E5M2), scales=t_scales[k][:], in_=dz_out[k][:])

        def turn_dz(k, copies):
            words = dz_out[k][:].bitcast(F32)
            f_in[k] = quantise_input()
            out = f_in[k][:].rearrange("q (p u e t) -> q p u e t", u=2, e=2, t=PACK)
            for u in range(2):
                bank = work_bank([P, PACK, P])
                for t in range(PACK):
                    nc.tensor.transpose(bank[:, t, :], words[:, 2 * P * t + u : 2 * P * (t + 1) : 2], ident[:])
                copies[u](out=out[:, :, u, :, :], in_=bank[:].bitcast(BF16).rearrange("q t (p e) -> q p e t", e=2))

        def quantise_features(k):
            cols = slice(k // NF * KG, (k // NF + 1) * KG)
            nc.vector.quantize_mx(
                out=f_codes[:, k % NF, cols].bitcast(E5M2), scales=f_scales[:, k % NF, cols], in_=f_in[k][:])

        def turn_w(a, g):
            raw, off = w_raw[a, g]
            words = raw[:].bitcast(F32)
            w_in[a, g] = quantise_input()
            out = w_in[a, g][:].bitcast(F32)
            for pair in range(TILES // 2):
                bank = work_bank([P, 2, 2, P])
                for i in range(2):
                    for u in range(2):
                        nc.tensor.transpose(
                            bank[:, u, i, :], words[:, 2 * pair + i, off // 2 + u : (off + KG) // 2 : 2], ident[:])
                nc.scalar.copy(
                    out=out[:, pair * KG : (pair + 1) * KG].rearrange("q (r u) -> q r u", u=2),
                    in_=bank[:].rearrange("q u i r -> q (i r) u"))

        def quantise_w(a, g):
            cols = slice(a * KG, (a + 1) * KG)
            nc.vector.quantize_mx(out=w_codes[:, g, cols].bitcast(E4M3), scales=w_scales[:, g, cols], in_=w_in[a, g][:])

        def weave_x(G, a):
            x_in[G, a] = quantise_input()
            nc.scalar.copy(
                out=x_in[G, a][:].rearrange("p (w j) -> p w j", j=PACK),
                in_=x_raw[G][:, :, a * KG : (a + 1) * KG].rearrange("p j w -> p w j"))

        def quantise_x(G, a):
            cols = slice(a * KG, (a + 1) * KG)
            nc.vector.quantize_mx(out=x_codes[:, G, cols].bitcast(E4M3), scales=x_scales[:, G, cols], in_=x_in[G, a][:])

        def negate_scalar(out, in_):
            nc.scalar.activation(out=out, in_=in_, func=ACT.Copy, scale=-1.0)

        def negate_vector(out, in_):
            nc.vector.tensor_scalar(out=out, in0=in_, scalar1=-1.0, scalar2=None, op0=MULT)

        def result_tile():
            t = pool.tile([P, KG], F32, name="result", tag="result", bufs=9)
            return t

        def add_out_0(G, a, groups, empty):
            cols = slice(a * KG, (a + 1) * KG)
            for m in range(TILES):
                rows = slice(G * KG + m * P, G * KG + (m + 1) * P)
                for g in groups:
                    if g == 0:
                        sums[G, a, m] = psum.tile([P, KG], F32, name="sums", tag="sums%d" % m)
                    nc.tensor.matmul_mx(
                        out=sums[G, a, m][:],
                        lhsT=f_codes[:, g, rows].bitcast(E5M2), lhsT_scale=f_scales[:, g, rows],
                        rhs=w_codes[:, g, cols].bitcast(E4M3), rhs_scale=w_scales[:, g, cols],
                        start=(g == 0), stop=(g == NF - 1))
                if NF - 1 in groups:
                    result = result_tile()
                    empty[m](result[:], sums[G, a, m][:])
                    nc.sync.dma_start(out=out_0_hbm[TILES * G + m, :, cols], in_=result[:])

        def make_out_1(g, hb, empty):
            bank = work_bank([P, KG])
            rows = slice(hb * P, (hb + 1) * P)
            for G in range(NG):
                k = G * NF + g
                nc.tensor.matmul_mx(
                    out=bank[:],
                    lhsT=x_codes[:, G, rows].bitcast(E4M3), lhsT_scale=x_scales[:, G, rows],
                    rhs=t_codes[k][:].bitcast(E5M2), rhs_scale=t_scales[k][:],
                    start=(G == 0), stop=(G == NG - 1))
            result = result_tile()
            empty(result[:].rearrange("p (q t) -> p q t", t=PACK), bank[:].rearrange("p (t q) -> p q t", t=PACK))
            nc.sync.dma_start(out=out_1_hbm[hb, :, g * KG : (g + 1) * KG], in_=result[:])

        scalar_four, both_four = [negate_scalar] * TILES, [negate_vector, negate_scalar] * (TILES // 2)

        nc.vector.memset(warm[:], 0.0)
        nc.scalar.activation(out=warm[:], in_=warm[:], func=ACT.Sigmoid)
        make_identity(nc, ident[:])
        load_z(0, HEAD_PARTS)
        load_grad(0, 0)
        load_z(1)
        load_w(0)
        load_z(2)
        load_w(1)
        load_rotation(0)
        load_gains()
        load_grad(1, 0)
        load_x(0)
        load_x(1)
        sigmoid(0, HEAD_PARTS)
        sigmoid(1)
        prepare_rotation()

        x_pieces = [(G, a) for G in range(NG) for a in range(HALVES)]
        quantised = turned = 0
        for k in range(NU):
            if k < 2:
                load_grad(k, 1)
            if 1 <= k <= 3:
                load_w(k + 1)
            derivative_b(k, HEAD_PARTS if k == 0 else 1)
            if k > 0:
                quantise_tokens(k - 1)
                for piece in w_pieces[quantised:turned]:
                    quantise_w(*piece)
                if k + 1 < NU:
                    sigmoid(k + 1)
            quantised = turned
            if 2 <= k <= len(x_pieces) + 1:
                quantise_x(*x_pieces[k - 2])
            turned = min(len(w_pieces), max(k + 1, 2 * k))
            for piece in w_pieces[quantised:turned]:
                turn_w(*piece)
            if k > NF:
                for hb in range(HB // 2):
                    make_out_1(k - NF - 1, hb, negate_scalar)
            derivative_c(k)
            if k + 3 < NU:
                load_z(k + 3)
            if k > 0:
                quantise_features(k - 1)
            if k > NF:
                for hb in range(HB // 2, HB):
                    make_out_1(k - NF - 1, hb, negate_scalar)
            if 1 <= k <= NF:
                add_out_0(0, 0, [k - 1], scalar_four)
            if k == NF + 1:
                add_out_0(0, 1, range(NF), scalar_four)
            if k == NF + 2:
                add_out_0(1, 0, range(2), scalar_four)
            if k > NF + 2:
                add_out_0(1, 0, [k - NF - 1], scalar_four)
            if 1 <= k <= len(x_pieces):
                weave_x(*x_pieces[k - 1])
            times_grad(k)
            if k < NU - 1:
                turn_dz(k, (nc.scalar.copy, nc.scalar.copy))
            if k == 2:
                turn_gains()
                rotate(0)
                load_rotation(1)
            if k == 3:
                turn_back(0)
                rotate(1)
            if k == 4:
                turn_back(1)

        quantise_tokens(NU - 1)
        turn_dz(NU - 1, (nc.scalar.copy, nc.vector.tensor_copy))
        quantise_features(NU - 1)
        add_out_0(1, 0, [NF - 1], both_four)
        for hb in range(HB):
            make_out_1(NF - 1, hb, (negate_vector, negate_scalar)[hb % 2])
        add_out_0(1, 1, range(NF), both_four)
